import numpy as np
import ml_dtypes


def mxq(x, axis, fmt="e4m3"):
    dtype, down = {"e4m3": (ml_dtypes.float8_e4m3fn, 7), "e5m2": (ml_dtypes.float8_e5m2, 14)}[fmt]
    v = np.moveaxis(np.asarray(x, np.float32).astype(ml_dtypes.bfloat16).astype(np.float64), axis, -1)
    blocks = v.reshape(v.shape[:-1] + (-1, 32))
    amax = np.abs(blocks).max(-1, keepdims=True)
    byte = np.maximum(np.where(amax > 0, np.frexp(amax)[1] - 1 + 127, 0) - down, 1)
    scale = np.exp2(byte - 127.0)
    codes = (blocks / scale).astype(np.float32).astype(dtype).astype(np.float64)
    return np.moveaxis((codes * scale).reshape(v.shape), -1, axis)


WIDE = False


def mx_kscale(k):
    if not WIDE:
        return np.ones(k)
    levels = np.array([10, -10, 5, -5, 0])
    a = np.random.permutation(np.resize(levels, k // 512 * 4)).reshape(k // 512, 4)
    idx = np.arange(k)
    return np.exp2(a[idx // 512, idx % 128 // 32])


BF16 = ml_dtypes.bfloat16


def bf(x):
    return np.asarray(x, np.float32).astype(BF16)


def f64(x):
    return np.asarray(x).astype(np.float64)


B, N, F, D, O = 2, 512, 1024, 128, 128


def setup_inputs():
    s = mx_kscale(F)
    return {"q": bf(np.random.standard_normal((B, N, D)) * 1.4),
            "k": bf(np.random.standard_normal((B, N, D)) * 1.4),
            "x": bf(np.random.standard_normal((B, N, F)) * s),
            "mask": bf(np.random.randint(0, 2, (B, N))),
            "weight": bf(np.random.standard_normal((F, O)) * 2.0 / np.sqrt(F) / s[:, None])}


def reference(q, k, x, mask, weight):
    sim = f64(q) @ f64(k).transpose(0, 2, 1) / np.sqrt(D)
    e = np.exp(sim - sim.max(-1, keepdims=True))
    support = mxq(f64(x), 2, "e4m3") @ mxq(f64(weight), 0, "e4m3")
    agg = mxq(e, 2, "e4m3") @ mxq(support, 1, "e4m3")
    return agg / e.sum(-1, keepdims=True) * f64(mask)[:, :, None]

@@ -1,0 +1,304 @@
+import math
+from contextlib import ExitStack
+
+import concourse.mybir as mybir
+from concourse.masks import make_identity
+
+F32 = mybir.dt.float32
+BF16 = mybir.dt.bfloat16
+U32 = mybir.dt.uint32
+U8 = mybir.dt.uint8
+FP8X4 = mybir.dt.float8_e4m3fn_x4
+ACT = mybir.ActivationFunctionType
+ALU = mybir.AluOpType
+AXIS = mybir.AxisListType
+
+P = 128
+PACK = 4
+GRAPHS, NODES, FEATS, DIM, OUT = 2, 512, 1024, 128, 128
+TILES = NODES // P
+ALL_TILES = GRAPHS * TILES
+PASSES = FEATS // (P * PACK)
+HALVES = 2
+SCALE = 1.0 / math.sqrt(DIM)
+
+FLOPS = 2 * GRAPHS * NODES * (NODES * DIM + FEATS * OUT + NODES * OUT)
+
+
+def tile_graphconvolution_wmask_learnadj_pa_s_kernel(tc, q, k, x, mask, weight, out):
+    nc = tc.nc
+    with ExitStack() as ctx:
+        keep = ctx.enter_context(tc.tile_pool(name="keep", bufs=1))
+        e_pool = ctx.enter_context(tc.tile_pool(name="e_pool", bufs=3))
+        ps_small = ctx.enter_context(tc.psum_pool(name="ps_small", bufs=2))
+        ps_x = ctx.enter_context(tc.psum_pool(name="ps_x", bufs=2))
+        ps_sim = ctx.enter_context(tc.psum_pool(name="ps_sim", bufs=2))
+        ps_mx = ctx.enter_context(tc.psum_pool(name="ps_mx", bufs=2))
+
+        q_rows = [keep.tile([P, TILES * DIM], BF16, name="q_rows%d" % b) for b in range(GRAPHS)]
+        k_rows = [keep.tile([P, TILES * DIM], BF16, name="k_rows%d" % b) for b in range(GRAPHS)]
+        x_rows = [keep.tile([P, TILES * FEATS], BF16, name="x_rows%d" % b) for b in range(GRAPHS)]
+        w_rows = keep.tile([P, PASSES, PACK, OUT], BF16, name="w_rows")
+        mask_bf = keep.tile([P, ALL_TILES], BF16, name="mask_bf")
+
+        qT = [keep.tile([P, NODES], BF16, name="qT%d" % b) for b in range(GRAPHS)]
+        kT = [keep.tile([P, NODES], BF16, name="kT%d" % b) for b in range(GRAPHS)]
+
+        w_grouped = keep.tile([P, PASSES * OUT * PACK], BF16, name="w_grouped", align_bytes=64)
+        w_codes = keep.tile([P, PASSES * OUT], U32, name="w_codes", align_bytes=64)
+        w_scales = keep.tile([P, PASSES * OUT], U8, name="w_scales", align_bytes=64)
+
+        x_grouped = [
+            keep.tile([P, TILES * FEATS], BF16, name="x_grouped%d" % b, align_bytes=64)
+            for b in range(GRAPHS)
+        ]
+        x_codes = [
+            keep.tile([P, TILES * FEATS // PACK], U32, name="x_codes%d" % b, align_bytes=64)
+            for b in range(GRAPHS)
+        ]
+        x_scales = [
+            keep.tile([P, TILES * FEATS // PACK], U8, name="x_scales%d" % b, align_bytes=64)
+            for b in range(GRAPHS)
+        ]
+
+        s_grouped = [
+            keep.tile([P, OUT * PACK], BF16, name="s_grouped%d" % b, align_bytes=64)
+            for b in range(GRAPHS)
+        ]
+        s_codes = [keep.tile([P, OUT], U32, name="s_codes%d" % b, align_bytes=64) for b in range(GRAPHS)]
+        s_scales = [keep.tile([P, OUT], U8, name="s_scales%d" % b, align_bytes=64) for b in range(GRAPHS)]
+
+        e_grouped = [
+            keep.tile([P, NODES * PACK], BF16, name="e_grouped%d" % b, align_bytes=64)
+            for b in range(GRAPHS)
+        ]
+        e_codes = [keep.tile([P, NODES], U32, name="e_codes%d" % b, align_bytes=64) for b in range(GRAPHS)]
+        e_scales = [keep.tile([P, NODES], U8, name="e_scales%d" % b, align_bytes=64) for b in range(GRAPHS)]
+
+        row_max = keep.tile([P, ALL_TILES], F32, name="row_max")
+        exp_bias = keep.tile([P, ALL_TILES], F32, name="exp_bias")
+        row_sum = keep.tile([P, ALL_TILES], F32, name="row_sum")
+        inv_sum = keep.tile([P, ALL_TILES], F32, name="inv_sum")
+        mask_f32 = keep.tile([P, ALL_TILES], F32, name="mask_f32")
+        out_rows = [keep.tile([P, TILES * OUT], F32, name="out_rows%d" % b) for b in range(GRAPHS)]
+
+        ident_bf = keep.tile([P, P], BF16, name="ident_bf")
+        ident_f32 = keep.tile([P, P], F32, name="ident_f32")
+        warm_in = keep.tile([P, 1], F32, name="warm_in")
+        warm_out = keep.tile([P, 1], F32, name="warm_out")
+
+        def load_qk(b):
+            nc.sync.dma_start(out=q_rows[b][:], in_=q[b].rearrange("(p t) d -> p (t d)", t=TILES))
+            nc.sync.dma_start(out=k_rows[b][:], in_=k[b].rearrange("(p t) d -> p (t d)", t=TILES))
+
+        def load_x(b, j):
+            nc.sync.dma_start(
+                out=x_rows[b][:, j * FEATS : (j + 1) * FEATS],
+                in_=x[b].rearrange("(p t) f -> p t f", t=TILES)[:, j, :],
+            )
+
+        nc.scalar.dma_start(
+            out=mask_bf[:].rearrange("p (b t) -> p b t", b=GRAPHS),
+            in_=mask.rearrange("b (p t) -> p b t", t=TILES),
+        )
+        load_qk(0)
+        load_x(0, 0)
+        load_x(0, 1)
+        nc.sync.dma_start(
+            out=w_rows[:].rearrange("p g (u e) o -> p (g u) (e o)", u=HALVES),
+            in_=weight.rearrange("(c p e) o -> p c (e o)", p=P, e=2),
+        )
+        load_x(0, 2)
+        load_x(0, 3)
+        load_qk(1)
+        for j in range(TILES):
+            load_x(1, j)
+
+        make_identity(nc, ident_bf[:])
+        make_identity(nc, ident_f32[:])
+        nc.vector.memset(warm_in[:], 0.0)
+        nc.scalar.activation(out=warm_out[:], in_=warm_in[:], func=ACT.Exp)
+
+        def qk_transposes(b):
+            qT_ps = ps_small.tile([P, TILES, P], BF16, tag="small")
+            for t in range(TILES):
+                nc.tensor.transpose(qT_ps[:, t, :], q_rows[b][:, t * DIM : (t + 1) * DIM], ident_bf[:])
+            nc.scalar.copy(out=qT[b][:], in_=qT_ps[:].rearrange("d t p -> d (t p)"))
+            kT_ps = ps_small.tile([P, TILES, P], BF16, tag="small")
+            for t in range(TILES):
+                nc.tensor.transpose(kT_ps[:, t, :], k_rows[b][:, t * DIM : (t + 1) * DIM], ident_bf[:])
+            nc.vector.tensor_copy(
+                out=kT[b][:].rearrange("d (u p e) -> d u p e", u=HALVES, e=2),
+                in_=kT_ps[:].rearrange("d (u e) p -> d u p e", u=HALVES),
+            )
+
+        def weight_quantise():
+            nc.vector.tensor_copy(
+                out=w_grouped[:].rearrange("p (g o t) -> p g o t", g=PASSES, t=PACK),
+                in_=w_rows[:].rearrange("p g t o -> p g o t"),
+            )
+            nc.vector.quantize_mx(out=w_codes[:].bitcast(FP8X4), scales=w_scales[:], in_=w_grouped[:])
+
+        xT_banks = {}
+
+        def x_transposes(c):
+            b, j = divmod(c, TILES)
+            words = x_rows[b][:].bitcast(F32)
+            xT_ps = ps_x.tile([P, PASSES * HALVES, P], F32, tag="xT")
+            for w in range(PASSES * HALVES):
+                first = (j * PASSES * HALVES + w) * P
+                nc.tensor.transpose(xT_ps[:, w, :], words[:, first : first + P], ident_f32[:])
+            xT_banks[c] = xT_ps
+
+        def x_copy(c):
+            b, j = divmod(c, TILES)
+            grouped_words = x_grouped[b][:].bitcast(F32).rearrange(
+                "p (j g m u) -> p j g m u", j=TILES, g=PASSES, u=HALVES
+            )
+            nc.scalar.copy(
+                out=grouped_words[:, j],
+                in_=xT_banks[c][:].rearrange("p (g u) m -> p g m u", u=HALVES),
+            )
+
+        def x_quantise(pair):
+            b, half = divmod(pair, TILES // 2)
+            width = 2 * FEATS
+            nc.vector.quantize_mx(
+                out=x_codes[b][:, half * width // PACK : (half + 1) * width // PACK].bitcast(FP8X4),
+                scales=x_scales[b][:, half * width // PACK : (half + 1) * width // PACK],
+                in_=x_grouped[b][:, half * width : (half + 1) * width],
+            )
+
+        def support(b):
+            sup_ps = ps_mx.tile([P, TILES, OUT], F32, tag="mx")
+            for j in range(TILES):
+                for g in range(PASSES):
+                    cols = slice((j * PASSES + g) * P, (j * PASSES + g + 1) * P)
+                    nc.tensor.matmul_mx(
+                        out=sup_ps[:, j, :],
+                        lhsT=x_codes[b][:, cols].bitcast(FP8X4),
+                        lhsT_scale=x_scales[b][:, cols],
+                        rhs=w_codes[:, g * OUT : (g + 1) * OUT].bitcast(FP8X4),
+                        rhs_scale=w_scales[:, g * OUT : (g + 1) * OUT],
+                        start=(g == 0),
+                        stop=(g == PASSES - 1),
+                    )
+            nc.scalar.copy(
+                out=s_grouped[b][:].rearrange("p (o j) -> p o j", j=PACK),
+                in_=sup_ps[:].rearrange("p j o -> p o j"),
+            )
+
+        def support_quantise(b):
+            nc.vector.quantize_mx(out=s_codes[b][:].bitcast(FP8X4), scales=s_scales[b][:], in_=s_grouped[b][:])
+
+        sim_banks = {}
+
+        def sim(s):
+            b, i = divmod(s, TILES)
+            sim_ps = ps_sim.tile([P, NODES], F32, tag="sim")
+            nc.tensor.matmul(sim_ps[:], lhsT=qT[b][:, i * P : (i + 1) * P], rhs=kT[b][:], start=True, stop=True)
+            sim_banks[s] = sim_ps
+
+        def softmax_max(s):
+            nc.vector.tensor_reduce(out=row_max[:, s : s + 1], in_=sim_banks[s][:], axis=AXIS.X, op=ALU.max)
+            nc.vector.tensor_scalar(
+                out=exp_bias[:, s : s + 1], in0=row_max[:, s : s + 1], scalar1=-SCALE, scalar2=None, op0=ALU.mult
+            )
+
+        e_tiles = {}
+
+        def softmax_exp(s):
+            e_rows = e_pool.tile([P, NODES], BF16, tag="e_rows")
+            nc.scalar.activation(
+                out=e_rows[:],
+                in_=sim_banks[s][:],
+                func=ACT.Exp,
+                bias=exp_bias[:, s : s + 1],
+                scale=SCALE,
+                accum_out=row_sum[:, s : s + 1],
+            )
+            e_tiles[s] = e_rows
+
+        eT_banks = {}
+
+        def e_transposes(s):
+            words = e_tiles[s][:].bitcast(F32)
+            eT_ps = ps_small.tile([P, HALVES, P], F32, tag="small")
+            for u in range(HALVES):
+                nc.tensor.transpose(eT_ps[:, u, :], words[:, u * P : (u + 1) * P], ident_f32[:])
+            eT_banks[s] = eT_ps
+
+        def e_copy(s):
+            b, i = divmod(s, TILES)
+            grouped_words = e_grouped[b][:].bitcast(F32).rearrange("p (i n u) -> p i n u", i=TILES, u=HALVES)
+            source = eT_banks[s][:].rearrange("p u n -> p n u")
+            if b == 0:
+                nc.vector.tensor_copy(out=grouped_words[:, i], in_=source)
+            else:
+                nc.scalar.copy(out=grouped_words[:, i], in_=source)
+
+        def e_quantise(s):
+            b, i = divmod(s, TILES)
+            nc.vector.quantize_mx(
+                out=e_codes[b][:, i * P : (i + 1) * P].bitcast(FP8X4),
+                scales=e_scales[b][:, i * P : (i + 1) * P],
+                in_=e_grouped[b][:, i * P * PACK : (i + 1) * P * PACK],
+            )
+            nc.vector.reciprocal(out=inv_sum[:, s : s + 1], in_=row_sum[:, s : s + 1])
+
+        def aggregate(s):
+            b, i = divmod(s, TILES)
+            agg_ps = ps_mx.tile([P, OUT], F32, tag="mx")
+            nc.tensor.matmul_mx(
+                out=agg_ps[:],
+                lhsT=e_codes[b][:, i * P : (i + 1) * P].bitcast(FP8X4),
+                lhsT_scale=e_scales[b][:, i * P : (i + 1) * P],
+                rhs=s_codes[b][:].bitcast(FP8X4),
+                rhs_scale=s_scales[b][:],
+                start=True,
+                stop=True,
+            )
+            nc.vector.tensor_scalar(
+                out=out_rows[b][:, i * OUT : (i + 1) * OUT],
+                in0=agg_ps[:],
+                scalar1=inv_sum[:, s : s + 1],
+                scalar2=mask_f32[:, s : s + 1],
+                op0=ALU.mult,
+                op1=ALU.mult,
+            )
+            if i == TILES - 1:
+                nc.sync.dma_start(out=out[b].rearrange("(p t) o -> p (t o)", t=TILES), in_=out_rows[b][:])
+
+        qk_transposes(0)
+        sim(0)
+        sim(1)
+        nc.vector.tensor_copy(out=mask_f32[:], in_=mask_bf[:])
+        for r in range(ALL_TILES + 3):
+            if r < ALL_TILES:
+                if r < TILES:
+                    x_transposes(2 * r)
+                    x_transposes(2 * r + 1)
+                if r == 2:
+                    qk_transposes(1)
+                softmax_max(r)
+                if r < TILES:
+                    x_copy(2 * r)
+                softmax_exp(r)
+                if r + 2 < ALL_TILES:
+                    sim(r + 2)
+                e_transposes(r)
+                if r < TILES:
+                    x_copy(2 * r + 1)
+            if r == 1:
+                weight_quantise()
+            if 1 <= r <= ALL_TILES:
+                e_copy(r - 1)
+                if r - 1 < TILES:
+                    x_quantise(r - 1)
+                e_quantise(r - 1)
+                if r == 2 or r == 4:
+                    support(r // 2 - 1)
+            if r >= 3:
+                if (r - 3) % TILES == 0:
+                    support_quantise((r - 3) // TILES)
+                aggregate(r - 3)

@@ -11,7 +11,6 @@ U8 = mybir.dt.uint8
 FP8X4 = mybir.dt.float8_e4m3fn_x4
 ACT = mybir.ActivationFunctionType
 ALU = mybir.AluOpType
-AXIS = mybir.AxisListType
 
 P = 128
 PACK = 4
@@ -30,10 +29,8 @@ def tile_graphconvolution_wmask_learnadj_pa_s_kernel(tc, q, k, x, mask, weight, 
     with ExitStack() as ctx:
         keep = ctx.enter_context(tc.tile_pool(name="keep", bufs=1))
         e_pool = ctx.enter_context(tc.tile_pool(name="e_pool", bufs=3))
-        ps_small = ctx.enter_context(tc.psum_pool(name="ps_small", bufs=2))
-        ps_x = ctx.enter_context(tc.psum_pool(name="ps_x", bufs=2))
-        ps_sim = ctx.enter_context(tc.psum_pool(name="ps_sim", bufs=2))
-        ps_mx = ctx.enter_context(tc.psum_pool(name="ps_mx", bufs=2))
+        ps_sim = ctx.enter_context(tc.psum_pool(name="ps_sim", bufs=3))
+        ps_short = ctx.enter_context(tc.psum_pool(name="ps_short", bufs=5))
 
         q_rows = [keep.tile([P, TILES * DIM], BF16, name="q_rows%d" % b) for b in range(GRAPHS)]
         k_rows = [keep.tile([P, TILES * DIM], BF16, name="k_rows%d" % b) for b in range(GRAPHS)]
@@ -75,7 +72,7 @@ def tile_graphconvolution_wmask_learnadj_pa_s_kernel(tc, q, k, x, mask, weight, 
         e_codes = [keep.tile([P, NODES], U32, name="e_codes%d" % b, align_bytes=64) for b in range(GRAPHS)]
         e_scales = [keep.tile([P, NODES], U8, name="e_scales%d" % b, align_bytes=64) for b in range(GRAPHS)]
 
-        row_max = keep.tile([P, ALL_TILES], F32, name="row_max")
+        scaled_sim = keep.tile([P, ALL_TILES * NODES], BF16, name="scaled_sim")
         exp_bias = keep.tile([P, ALL_TILES], F32, name="exp_bias")
         row_sum = keep.tile([P, ALL_TILES], F32, name="row_sum")
         inv_sum = keep.tile([P, ALL_TILES], F32, name="inv_sum")
@@ -87,44 +84,28 @@ def tile_graphconvolution_wmask_learnadj_pa_s_kernel(tc, q, k, x, mask, weight, 
         warm_in = keep.tile([P, 1], F32, name="warm_in")
         warm_out = keep.tile([P, 1], F32, name="warm_out")
 
-        def load_qk(b):
-            nc.sync.dma_start(out=q_rows[b][:], in_=q[b].rearrange("(p t) d -> p (t d)", t=TILES))
-            nc.sync.dma_start(out=k_rows[b][:], in_=k[b].rearrange("(p t) d -> p (t d)", t=TILES))
+        xT_banks = {}
+        sim_banks = {}
+        e_tiles = {}
+        eT_banks = {}
+        sup_banks = {}
+        agg_banks = {}
 
-        def load_x(b, j):
+        def load_x(c):
+            b, j = divmod(c, TILES)
             nc.sync.dma_start(
                 out=x_rows[b][:, j * FEATS : (j + 1) * FEATS],
                 in_=x[b].rearrange("(p t) f -> p t f", t=TILES)[:, j, :],
             )
 
-        nc.scalar.dma_start(
-            out=mask_bf[:].rearrange("p (b t) -> p b t", b=GRAPHS),
-            in_=mask.rearrange("b (p t) -> p b t", t=TILES),
-        )
-        load_qk(0)
-        load_x(0, 0)
-        load_x(0, 1)
-        nc.sync.dma_start(
-            out=w_rows[:].rearrange("p g (u e) o -> p (g u) (e o)", u=HALVES),
-            in_=weight.rearrange("(c p e) o -> p c (e o)", p=P, e=2),
-        )
-        load_x(0, 2)
-        load_x(0, 3)
-        load_qk(1)
-        for j in range(TILES):
-            load_x(1, j)
-
-        make_identity(nc, ident_bf[:])
-        make_identity(nc, ident_f32[:])
-        nc.vector.memset(warm_in[:], 0.0)
-        nc.scalar.activation(out=warm_out[:], in_=warm_in[:], func=ACT.Exp)
-
-        def qk_transposes(b):
-            qT_ps = ps_small.tile([P, TILES, P], BF16, tag="small")
+        def q_transposes(b):
+            qT_ps = ps_short.tile([P, TILES, P], BF16, tag="bank")
             for t in range(TILES):
                 nc.tensor.transpose(qT_ps[:, t, :], q_rows[b][:, t * DIM : (t + 1) * DIM], ident_bf[:])
             nc.scalar.copy(out=qT[b][:], in_=qT_ps[:].rearrange("d t p -> d (t p)"))
-            kT_ps = ps_small.tile([P, TILES, P], BF16, tag="small")
+
+        def k_transposes(b):
+            kT_ps = ps_short.tile([P, TILES, P], BF16, tag="bank")
             for t in range(TILES):
                 nc.tensor.transpose(kT_ps[:, t, :], k_rows[b][:, t * DIM : (t + 1) * DIM], ident_bf[:])
             nc.vector.tensor_copy(
@@ -139,12 +120,10 @@ def tile_graphconvolution_wmask_learnadj_pa_s_kernel(tc, q, k, x, mask, weight, 
             )
             nc.vector.quantize_mx(out=w_codes[:].bitcast(FP8X4), scales=w_scales[:], in_=w_grouped[:])
 
-        xT_banks = {}
-
         def x_transposes(c):
             b, j = divmod(c, TILES)
             words = x_rows[b][:].bitcast(F32)
-            xT_ps = ps_x.tile([P, PASSES * HALVES, P], F32, tag="xT")
+            xT_ps = ps_short.tile([P, PASSES * HALVES, P], F32, tag="bank")
             for w in range(PASSES * HALVES):
                 first = (j * PASSES * HALVES + w) * P
                 nc.tensor.transpose(xT_ps[:, w, :], words[:, first : first + P], ident_f32[:])
@@ -169,8 +148,8 @@ def tile_graphconvolution_wmask_learnadj_pa_s_kernel(tc, q, k, x, mask, weight, 
                 in_=x_grouped[b][:, half * width : (half + 1) * width],
             )
 
-        def support(b):
-            sup_ps = ps_mx.tile([P, TILES, OUT], F32, tag="mx")
+        def support_passes(b):
+            sup_ps = ps_short.tile([P, TILES, OUT], F32, tag="bank")
             for j in range(TILES):
                 for g in range(PASSES):
                     cols = slice((j * PASSES + g) * P, (j * PASSES + g + 1) * P)
@@ -183,29 +162,33 @@ def tile_graphconvolution_wmask_learnadj_pa_s_kernel(tc, q, k, x, mask, weight, 
                         start=(g == 0),
                         stop=(g == PASSES - 1),
                     )
+            sup_banks[b] = sup_ps
+
+        def support_copy(b):
             nc.scalar.copy(
                 out=s_grouped[b][:].rearrange("p (o j) -> p o j", j=PACK),
-                in_=sup_ps[:].rearrange("p j o -> p o j"),
+                in_=sup_banks[b][:].rearrange("p j o -> p o j"),
             )
 
         def support_quantise(b):
             nc.vector.quantize_mx(out=s_codes[b][:].bitcast(FP8X4), scales=s_scales[b][:], in_=s_grouped[b][:])
 
-        sim_banks = {}
-
         def sim(s):
             b, i = divmod(s, TILES)
-            sim_ps = ps_sim.tile([P, NODES], F32, tag="sim")
+            sim_ps = ps_sim.tile([P, NODES], F32, tag="bank")
             nc.tensor.matmul(sim_ps[:], lhsT=qT[b][:, i * P : (i + 1) * P], rhs=kT[b][:], start=True, stop=True)
             sim_banks[s] = sim_ps
 
         def softmax_max(s):
-            nc.vector.tensor_reduce(out=row_max[:, s : s + 1], in_=sim_banks[s][:], axis=AXIS.X, op=ALU.max)
             nc.vector.tensor_scalar(
-                out=exp_bias[:, s : s + 1], in0=row_max[:, s : s + 1], scalar1=-SCALE, scalar2=None, op0=ALU.mult
+                out=scaled_sim[:, s * NODES : (s + 1) * NODES],
+                in0=sim_banks[s][:],
+                scalar1=-SCALE,
+                scalar2=None,
+                op0=ALU.mult,
+                op1=ALU.min,
+                accum_out=exp_bias[:, s : s + 1],
             )
-
-        e_tiles = {}
 
         def softmax_exp(s):
             e_rows = e_pool.tile([P, NODES], BF16, tag="e_rows")
@@ -219,11 +202,9 @@ def tile_graphconvolution_wmask_learnadj_pa_s_kernel(tc, q, k, x, mask, weight, 
             )
             e_tiles[s] = e_rows
 
-        eT_banks = {}
-
         def e_transposes(s):
             words = e_tiles[s][:].bitcast(F32)
-            eT_ps = ps_small.tile([P, HALVES, P], F32, tag="small")
+            eT_ps = ps_short.tile([P, HALVES, P], F32, tag="bank")
             for u in range(HALVES):
                 nc.tensor.transpose(eT_ps[:, u, :], words[:, u * P : (u + 1) * P], ident_f32[:])
             eT_banks[s] = eT_ps
@@ -244,11 +225,10 @@ def tile_graphconvolution_wmask_learnadj_pa_s_kernel(tc, q, k, x, mask, weight, 
                 scales=e_scales[b][:, i * P : (i + 1) * P],
                 in_=e_grouped[b][:, i * P * PACK : (i + 1) * P * PACK],
             )
-            nc.vector.reciprocal(out=inv_sum[:, s : s + 1], in_=row_sum[:, s : s + 1])
 
         def aggregate(s):
             b, i = divmod(s, TILES)
-            agg_ps = ps_mx.tile([P, OUT], F32, tag="mx")
+            agg_ps = ps_short.tile([P, OUT], F32, tag="bank")
             nc.tensor.matmul_mx(
                 out=agg_ps[:],
                 lhsT=e_codes[b][:, i * P : (i + 1) * P].bitcast(FP8X4),
@@ -258,47 +238,93 @@ def tile_graphconvolution_wmask_learnadj_pa_s_kernel(tc, q, k, x, mask, weight, 
                 start=True,
                 stop=True,
             )
+            agg_banks[s] = agg_ps
+
+        def invert_sums(b):
+            nc.vector.reciprocal(
+                out=inv_sum[:, b * TILES : (b + 1) * TILES], in_=row_sum[:, b * TILES : (b + 1) * TILES]
+            )
+
+        def scale_and_store(s):
+            b, i = divmod(s, TILES)
             nc.vector.tensor_scalar(
                 out=out_rows[b][:, i * OUT : (i + 1) * OUT],
-                in0=agg_ps[:],
+                in0=agg_banks[s][:],
                 scalar1=inv_sum[:, s : s + 1],
                 scalar2=mask_f32[:, s : s + 1],
                 op0=ALU.mult,
                 op1=ALU.mult,
             )
-            if i == TILES - 1:
-                nc.sync.dma_start(out=out[b].rearrange("(p t) o -> p (t o)", t=TILES), in_=out_rows[b][:])
+            if i % 2 == 1:
+                nc.sync.dma_start(
+                    out=out[b].rearrange("(p t) o -> p t o", t=TILES)[:, i - 1 : i + 1, :],
+                    in_=out_rows[b][:, (i - 1) * OUT : (i + 1) * OUT].rearrange("p (t o) -> p t o", t=2),
+                )
 
-        qk_transposes(0)
-        sim(0)
-        sim(1)
+        def is_tile(s):
+            return 0 <= s < ALL_TILES
+
+        def chunks_of_round(r):
+            return [c for c in (2 * (r + 1), 2 * (r + 1) + 1) if 0 <= c < ALL_TILES]
+
+        nc.scalar.dma_start(
+            out=mask_bf[:].rearrange("p (b t) -> p b t", b=GRAPHS),
+            in_=mask.rearrange("b (p t) -> p b t", t=TILES),
+        )
+        for b in range(GRAPHS):
+            nc.sync.dma_start(out=q_rows[b][:], in_=q[b].rearrange("(p t) d -> p (t d)", t=TILES))
+            nc.sync.dma_start(out=k_rows[b][:], in_=k[b].rearrange("(p t) d -> p (t d)", t=TILES))
+        nc.sync.dma_start(
+            out=w_rows[:].rearrange("p g (u e) o -> p (g u) (e o)", u=HALVES),
+            in_=weight.rearrange("(c p e) o -> p c (e o)", p=P, e=2),
+        )
+        for c in range(ALL_TILES):
+            load_x(c)
+
+        make_identity(nc, ident_bf[:])
+        make_identity(nc, ident_f32[:])
+        nc.vector.memset(warm_in[:], 0.0)
+        nc.scalar.activation(out=warm_out[:], in_=warm_in[:], func=ACT.Exp)
+
+        for b in range(GRAPHS):
+            q_transposes(b)
+            k_transposes(b)
+        for s in range(3):
+            sim(s)
+        weight_quantise()
         nc.vector.tensor_copy(out=mask_f32[:], in_=mask_bf[:])
-        for r in range(ALL_TILES + 3):
-            if r < ALL_TILES:
-                if r < TILES:
-                    x_transposes(2 * r)
-                    x_transposes(2 * r + 1)
-                if r == 2:
-                    qk_transposes(1)
+        for c in chunks_of_round(-1):
+            x_transposes(c)
+
+        for r in range(-1, ALL_TILES + 5):
+            if is_tile(r - 1):
+                softmax_exp(r - 1)
+            if is_tile(r):
                 softmax_max(r)
-                if r < TILES:
-                    x_copy(2 * r)
-                softmax_exp(r)
-                if r + 2 < ALL_TILES:
+            if is_tile(r - 1):
+                e_transposes(r - 1)
+                if is_tile(r + 2):
                     sim(r + 2)
-                e_transposes(r)
-                if r < TILES:
-                    x_copy(2 * r + 1)
-            if r == 1:
-                weight_quantise()
-            if 1 <= r <= ALL_TILES:
-                e_copy(r - 1)
-                if r - 1 < TILES:
-                    x_quantise(r - 1)
-                e_quantise(r - 1)
-                if r == 2 or r == 4:
-                    support(r // 2 - 1)
-            if r >= 3:
-                if (r - 3) % TILES == 0:
-                    support_quantise((r - 3) // TILES)
+            if is_tile(r - 2):
+                e_copy(r - 2)
+            for b in range(GRAPHS):
+                if r == 2 * b + 2:
+                    support_copy(b)
+                if r == 2 * b + 3:
+                    support_quantise(b)
+            if is_tile(r - 3):
+                e_quantise(r - 3)
                 aggregate(r - 3)
+            for c in chunks_of_round(r):
+                x_copy(c)
+            for c in chunks_of_round(r + 1):
+                x_transposes(c)
+            if chunks_of_round(r - 1):
+                x_quantise(r)
+            for b in range(GRAPHS):
+                if r == 2 * b + 1:
+                    support_passes(b)
+                if r == TILES * (b + 1):
+                    invert_sums(b)
+            if is_tile(r - 4):
+                scale_and_store(r - 4)

@@ -139,13 +139,12 @@ def tile_graphconvolution_wmask_learnadj_pa_s_kernel(tc, q, k, x, mask, weight, 
                 in_=xT_banks[c][:].rearrange("p (g u) m -> p g m u", u=HALVES),
             )
 
-        def x_quantise(pair):
-            b, half = divmod(pair, TILES // 2)
-            width = 2 * FEATS
+        def x_quantise(c):
+            b, j = divmod(c, TILES)
             nc.vector.quantize_mx(
-                out=x_codes[b][:, half * width // PACK : (half + 1) * width // PACK].bitcast(FP8X4),
-                scales=x_scales[b][:, half * width // PACK : (half + 1) * width // PACK],
-                in_=x_grouped[b][:, half * width : (half + 1) * width],
+                out=x_codes[b][:, j * FEATS // PACK : (j + 1) * FEATS // PACK].bitcast(FP8X4),
+                scales=x_scales[b][:, j * FEATS // PACK : (j + 1) * FEATS // PACK],
+                in_=x_grouped[b][:, j * FEATS : (j + 1) * FEATS],
             )
 
         def support_passes(b):
@@ -213,10 +212,7 @@ def tile_graphconvolution_wmask_learnadj_pa_s_kernel(tc, q, k, x, mask, weight, 
             b, i = divmod(s, TILES)
             grouped_words = e_grouped[b][:].bitcast(F32).rearrange("p (i n u) -> p i n u", i=TILES, u=HALVES)
             source = eT_banks[s][:].rearrange("p u n -> p n u")
-            if b == 0:
-                nc.vector.tensor_copy(out=grouped_words[:, i], in_=source)
-            else:
-                nc.scalar.copy(out=grouped_words[:, i], in_=source)
+            nc.vector.tensor_copy(out=grouped_words[:, i], in_=source)
 
         def e_quantise(s):
             b, i = divmod(s, TILES)
@@ -264,67 +260,77 @@ def tile_graphconvolution_wmask_learnadj_pa_s_kernel(tc, q, k, x, mask, weight, 
         def is_tile(s):
             return 0 <= s < ALL_TILES
 
-        def chunks_of_round(r):
-            return [c for c in (2 * (r + 1), 2 * (r + 1) + 1) if 0 <= c < ALL_TILES]
+        def product_round(s):
+            return max(s + 3, TILES * (s // TILES) + 4)
 
-        nc.scalar.dma_start(
-            out=mask_bf[:].rearrange("p (b t) -> p b t", b=GRAPHS),
-            in_=mask.rearrange("b (p t) -> p b t", t=TILES),
-        )
-        for b in range(GRAPHS):
-            nc.sync.dma_start(out=q_rows[b][:], in_=q[b].rearrange("(p t) d -> p (t d)", t=TILES))
-            nc.sync.dma_start(out=k_rows[b][:], in_=k[b].rearrange("(p t) d -> p (t d)", t=TILES))
-        nc.sync.dma_start(
-            out=w_rows[:].rearrange("p g (u e) o -> p (g u) (e o)", u=HALVES),
-            in_=weight.rearrange("(c p e) o -> p c (e o)", p=P, e=2),
-        )
-        for c in range(ALL_TILES):
-            load_x(c)
-
-        make_identity(nc, ident_bf[:])
-        make_identity(nc, ident_f32[:])
-        nc.vector.memset(warm_in[:], 0.0)
-        nc.scalar.activation(out=warm_out[:], in_=warm_in[:], func=ACT.Exp)
-
-        for b in range(GRAPHS):
-            q_transposes(b)
-            k_transposes(b)
-        for s in range(3):
-            sim(s)
-        weight_quantise()
-        nc.vector.tensor_copy(out=mask_f32[:], in_=mask_bf[:])
-        for c in chunks_of_round(-1):
-            x_transposes(c)
-
-        for r in range(-1, ALL_TILES + 5):
-            if is_tile(r - 1):
-                softmax_exp(r - 1)
-            if is_tile(r):
-                softmax_max(r)
-            if is_tile(r - 1):
-                e_transposes(r - 1)
-                if is_tile(r + 2):
-                    sim(r + 2)
-            if is_tile(r - 2):
-                e_copy(r - 2)
+        with tc.manual_schedule():
+            nc.scalar.dma_start(
+                out=mask_bf[:].rearrange("p (b t) -> p b t", b=GRAPHS),
+                in_=mask.rearrange("b (p t) -> p b t", t=TILES),
+            )
             for b in range(GRAPHS):
-                if r == 2 * b + 2:
-                    support_copy(b)
-                if r == 2 * b + 3:
-                    support_quantise(b)
-            if is_tile(r - 3):
-                e_quantise(r - 3)
-                aggregate(r - 3)
-            for c in chunks_of_round(r):
-                x_copy(c)
-            for c in chunks_of_round(r + 1):
-                x_transposes(c)
-            if chunks_of_round(r - 1):
-                x_quantise(r)
+                nc.sync.dma_start(out=q_rows[b][:], in_=q[b].rearrange("(p t) d -> p (t d)", t=TILES))
+                nc.sync.dma_start(out=k_rows[b][:], in_=k[b].rearrange("(p t) d -> p (t d)", t=TILES))
+            load_x(0)
+            load_x(1)
+            nc.sync.dma_start(
+                out=w_rows[:].rearrange("p g (u e) o -> p (g u) (e o)", u=HALVES),
+                in_=weight.rearrange("(c p e) o -> p c (e o)", p=P, e=2),
+            )
+            for c in range(2, ALL_TILES):
+                load_x(c)
+
+            make_identity(nc, ident_bf[:])
+            make_identity(nc, ident_f32[:])
+            nc.vector.memset(warm_in[:], 0.0)
+            nc.scalar.activation(out=warm_out[:], in_=warm_in[:], func=ACT.Exp)
+
             for b in range(GRAPHS):
-                if r == 2 * b + 1:
-                    support_passes(b)
-                if r == TILES * (b + 1):
-                    invert_sums(b)
-            if is_tile(r - 4):
-                scale_and_store(r - 4)
+                q_transposes(b)
+                k_transposes(b)
+            x_transposes(0)
+            for s in range(3):
+                sim(s)
+            nc.vector.tensor_copy(out=mask_f32[:], in_=mask_bf[:])
+
+            for r in range(-2, ALL_TILES + 4):
+                c = r + 2
+                if is_tile(r):
+                    softmax_exp(r)
+                if is_tile(c):
+                    x_copy(c)
+                for b in range(GRAPHS):
+                    if r == TILES * b + 3:
+                        support_copy(b)
+
+                if is_tile(c + 1):
+                    x_transposes(c + 1)
+                if is_tile(r):
+                    e_transposes(r)
+                    if is_tile(r + 3):
+                        sim(r + 3)
+
+                if is_tile(r + 1):
+                    softmax_max(r + 1)
+                if r == -1:
+                    weight_quantise()
+                if is_tile(r - 1):
+                    e_copy(r - 1)
+                if is_tile(c - 1):
+                    x_quantise(c - 1)
+                for b in range(GRAPHS):
+                    if r == TILES * b + 2:
+                        support_passes(b)
+                    if r == TILES * b + 4:
+                        support_quantise(b)
+                if is_tile(r - 2):
+                    e_quantise(r - 2)
+                for s in range(ALL_TILES):
+                    if product_round(s) == r:
+                        aggregate(s)
+                for b in range(GRAPHS):
+                    if r == TILES * b + 4:
+                        invert_sums(b)
+                for s in range(ALL_TILES):
+                    if product_round(s) + 1 == r:
+                        scale_and_store(s)

@@ -18,6 +18,7 @@ GRAPHS, NODES, FEATS, DIM, OUT = 2, 512, 1024, 128, 128
 TILES = NODES // P
 ALL_TILES = GRAPHS * TILES
 PASSES = FEATS // (P * PACK)
+BUSY_N = 256
 HALVES = 2
 SCALE = 1.0 / math.sqrt(DIM)
 
@@ -81,6 +82,9 @@ def tile_graphconvolution_wmask_learnadj_pa_s_kernel(tc, q, k, x, mask, weight, 
 
         ident_bf = keep.tile([P, P], BF16, name="ident_bf")
         ident_f32 = keep.tile([P, P], F32, name="ident_f32")
+        busy_ones = keep.tile([P, BUSY_N * PACK], BF16, name="busy_ones", align_bytes=64)
+        busy_codes = keep.tile([P, BUSY_N], U32, name="busy_codes", align_bytes=64)
+        busy_scales = keep.tile([P, BUSY_N], U8, name="busy_scales", align_bytes=64)
         warm_in = keep.tile([P, 1], F32, name="warm_in")
         warm_out = keep.tile([P, 1], F32, name="warm_out")
 
@@ -172,11 +176,23 @@ def tile_graphconvolution_wmask_learnadj_pa_s_kernel(tc, q, k, x, mask, weight, 
         def support_quantise(b):
             nc.vector.quantize_mx(out=s_codes[b][:].bitcast(FP8X4), scales=s_scales[b][:], in_=s_grouped[b][:])
 
+        def busy_passes(s, count):
+            sim_banks[s] = ps_sim.tile([P, NODES], F32, tag="bank", name="sim_ps")
+            for repeat in range(count):
+                nc.tensor.matmul_mx(
+                    out=sim_banks[s][:, :BUSY_N],
+                    lhsT=busy_codes[:, :P].bitcast(FP8X4),
+                    lhsT_scale=busy_scales[:, :P],
+                    rhs=busy_codes[:].bitcast(FP8X4),
+                    rhs_scale=busy_scales[:],
+                    start=True,
+                    stop=True,
+                )
+
         def sim(s):
             b, i = divmod(s, TILES)
-            sim_ps = ps_sim.tile([P, NODES], F32, tag="bank")
+            sim_ps = sim_banks[s]
             nc.tensor.matmul(sim_ps[:], lhsT=qT[b][:, i * P : (i + 1) * P], rhs=kT[b][:], start=True, stop=True)
-            sim_banks[s] = sim_ps
 
         def softmax_max(s):
             nc.vector.tensor_scalar(
@@ -283,13 +299,18 @@ def tile_graphconvolution_wmask_learnadj_pa_s_kernel(tc, q, k, x, mask, weight, 
             make_identity(nc, ident_bf[:])
             make_identity(nc, ident_f32[:])
             nc.vector.memset(warm_in[:], 0.0)
+            nc.vector.memset(busy_ones[:], 1.0)
+            nc.vector.quantize_mx(out=busy_codes[:].bitcast(FP8X4), scales=busy_scales[:], in_=busy_ones[:])
+            busy_passes(0, 6)
             nc.scalar.activation(out=warm_out[:], in_=warm_in[:], func=ACT.Exp)
 
             for b in range(GRAPHS):
                 q_transposes(b)
                 k_transposes(b)
             x_transposes(0)
-            for s in range(3):
+            sim(0)
+            for s in range(1, 3):
+                busy_passes(s, 1)
                 sim(s)
             nc.vector.tensor_copy(out=mask_f32[:], in_=mask_bf[:])
 
@@ -307,6 +328,7 @@ def tile_graphconvolution_wmask_learnadj_pa_s_kernel(tc, q, k, x, mask, weight, 
                     x_transposes(c + 1)
                 if is_tile(r):
                     e_transposes(r)
+                    busy_passes(r + 3, 2)
                     if is_tile(r + 3):
                         sim(r + 3)
 

@@ -16,9 +16,11 @@ P = 128
 PACK = 4
 GRAPHS, NODES, FEATS, DIM, OUT = 2, 512, 1024, 128, 128
 TILES = NODES // P
+ON_SCALAR_E = (1, 3)
+ON_VECTOR_OUT = (5, 7)
 ALL_TILES = GRAPHS * TILES
 PASSES = FEATS // (P * PACK)
-BUSY_N = 256
+BUSY_N = 128
 HALVES = 2
 SCALE = 1.0 / math.sqrt(DIM)
 
@@ -30,8 +32,8 @@ def tile_graphconvolution_wmask_learnadj_pa_s_kernel(tc, q, k, x, mask, weight, 
     with ExitStack() as ctx:
         keep = ctx.enter_context(tc.tile_pool(name="keep", bufs=1))
         e_pool = ctx.enter_context(tc.tile_pool(name="e_pool", bufs=3))
-        ps_sim = ctx.enter_context(tc.psum_pool(name="ps_sim", bufs=3))
-        ps_short = ctx.enter_context(tc.psum_pool(name="ps_short", bufs=5))
+        ps_sim = ctx.enter_context(tc.psum_pool(name="ps_sim", bufs=2))
+        ps_short = ctx.enter_context(tc.psum_pool(name="ps_short", bufs=6))
 
         q_rows = [keep.tile([P, TILES * DIM], BF16, name="q_rows%d" % b) for b in range(GRAPHS)]
         k_rows = [keep.tile([P, TILES * DIM], BF16, name="k_rows%d" % b) for b in range(GRAPHS)]
@@ -73,16 +75,17 @@ def tile_graphconvolution_wmask_learnadj_pa_s_kernel(tc, q, k, x, mask, weight, 
         e_codes = [keep.tile([P, NODES], U32, name="e_codes%d" % b, align_bytes=64) for b in range(GRAPHS)]
         e_scales = [keep.tile([P, NODES], U8, name="e_scales%d" % b, align_bytes=64) for b in range(GRAPHS)]
 
-        scaled_sim = keep.tile([P, ALL_TILES * NODES], BF16, name="scaled_sim")
+        scaled_sim = keep.tile([P, ALL_TILES * NODES], F32, name="scaled_sim")
         exp_bias = keep.tile([P, ALL_TILES], F32, name="exp_bias")
         row_sum = keep.tile([P, ALL_TILES], F32, name="row_sum")
         inv_sum = keep.tile([P, ALL_TILES], F32, name="inv_sum")
+        factor = keep.tile([P, ALL_TILES], F32, name="factor")
         mask_f32 = keep.tile([P, ALL_TILES], F32, name="mask_f32")
         out_rows = [keep.tile([P, TILES * OUT], F32, name="out_rows%d" % b) for b in range(GRAPHS)]
 
         ident_bf = keep.tile([P, P], BF16, name="ident_bf")
         ident_f32 = keep.tile([P, P], F32, name="ident_f32")
-        busy_ones = keep.tile([P, BUSY_N * PACK], BF16, name="busy_ones", align_bytes=64)
+        busy_zeros = keep.tile([P, BUSY_N * PACK], BF16, name="busy_zeros", align_bytes=64)
         busy_codes = keep.tile([P, BUSY_N], U32, name="busy_codes", align_bytes=64)
         busy_scales = keep.tile([P, BUSY_N], U8, name="busy_scales", align_bytes=64)
         warm_in = keep.tile([P, 1], F32, name="warm_in")
@@ -117,11 +120,17 @@ def tile_graphconvolution_wmask_learnadj_pa_s_kernel(tc, q, k, x, mask, weight, 
                 in_=kT_ps[:].rearrange("d (u e) p -> d u p e", u=HALVES),
             )
 
-        def weight_quantise():
-            nc.vector.tensor_copy(
+        def weight_interleave():
+            nc.gpsimd.tensor_scalar(
                 out=w_grouped[:].rearrange("p (g o t) -> p g o t", g=PASSES, t=PACK),
-                in_=w_rows[:].rearrange("p g t o -> p g o t"),
+                in0=w_rows[:].rearrange("p g t o -> p g o t"),
+                scalar1=1.0,
+                scalar2=0.0,
+                op0=ALU.mult,
+                op1=ALU.add,
             )
+
+        def weight_quantise():
             nc.vector.quantize_mx(out=w_codes[:].bitcast(FP8X4), scales=w_scales[:], in_=w_grouped[:])
 
         def x_transposes(c):
@@ -176,11 +185,10 @@ def tile_graphconvolution_wmask_learnadj_pa_s_kernel(tc, q, k, x, mask, weight, 
         def support_quantise(b):
             nc.vector.quantize_mx(out=s_codes[b][:].bitcast(FP8X4), scales=s_scales[b][:], in_=s_grouped[b][:])
 
-        def busy_passes(s, count):
-            sim_banks[s] = ps_sim.tile([P, NODES], F32, tag="bank", name="sim_ps")
+        def busy_passes(bank, count):
             for repeat in range(count):
                 nc.tensor.matmul_mx(
-                    out=sim_banks[s][:, :BUSY_N],
+                    out=bank[:, :BUSY_N],
                     lhsT=busy_codes[:, :P].bitcast(FP8X4),
                     lhsT_scale=busy_scales[:, :P],
                     rhs=busy_codes[:].bitcast(FP8X4),
@@ -189,10 +197,12 @@ def tile_graphconvolution_wmask_learnadj_pa_s_kernel(tc, q, k, x, mask, weight, 
                     stop=True,
                 )
 
-        def sim(s):
+        def sim(s, busy):
             b, i = divmod(s, TILES)
-            sim_ps = sim_banks[s]
+            sim_ps = ps_sim.tile([P, NODES], F32, tag="bank")
+            busy_passes(sim_ps, busy)
             nc.tensor.matmul(sim_ps[:], lhsT=qT[b][:, i * P : (i + 1) * P], rhs=kT[b][:], start=True, stop=True)
+            sim_banks[s] = sim_ps
 
         def softmax_max(s):
             nc.vector.tensor_scalar(
@@ -209,10 +219,10 @@ def tile_graphconvolution_wmask_learnadj_pa_s_kernel(tc, q, k, x, mask, weight, 
             e_rows = e_pool.tile([P, NODES], BF16, tag="e_rows")
             nc.scalar.activation(
                 out=e_rows[:],
-                in_=sim_banks[s][:],
+                in_=scaled_sim[:, s * NODES : (s + 1) * NODES],
                 func=ACT.Exp,
                 bias=exp_bias[:, s : s + 1],
-                scale=SCALE,
+                scale=-1.0,
                 accum_out=row_sum[:, s : s + 1],
             )
             e_tiles[s] = e_rows
@@ -226,9 +236,10 @@ def tile_graphconvolution_wmask_learnadj_pa_s_kernel(tc, q, k, x, mask, weight, 
 
         def e_copy(s):
             b, i = divmod(s, TILES)
+            copy = nc.scalar.copy if s in ON_SCALAR_E else nc.vector.tensor_copy
             grouped_words = e_grouped[b][:].bitcast(F32).rearrange("p (i n u) -> p i n u", i=TILES, u=HALVES)
             source = eT_banks[s][:].rearrange("p u n -> p n u")
-            nc.vector.tensor_copy(out=grouped_words[:, i], in_=source)
+            copy(out=grouped_words[:, i], in_=source)
 
         def e_quantise(s):
             b, i = divmod(s, TILES)
@@ -240,9 +251,14 @@ def tile_graphconvolution_wmask_learnadj_pa_s_kernel(tc, q, k, x, mask, weight, 
 
         def aggregate(s):
             b, i = divmod(s, TILES)
-            agg_ps = ps_short.tile([P, OUT], F32, tag="bank")
+            if s < TILES:
+                if s == 0:
+                    agg_banks["first"] = ps_short.tile([P, TILES, OUT], F32, tag="bank", name="agg_ps")
+                agg_ps = agg_banks["first"][:, i, :]
+            else:
+                agg_ps = ps_short.tile([P, OUT], F32, tag="bank", name="agg_one")[:]
             nc.tensor.matmul_mx(
-                out=agg_ps[:],
+                out=agg_ps,
                 lhsT=e_codes[b][:, i * P : (i + 1) * P].bitcast(FP8X4),
                 lhsT_scale=e_scales[b][:, i * P : (i + 1) * P],
                 rhs=s_codes[b][:].bitcast(FP8X4),
@@ -256,17 +272,30 @@ def tile_graphconvolution_wmask_learnadj_pa_s_kernel(tc, q, k, x, mask, weight, 
             nc.vector.reciprocal(
                 out=inv_sum[:, b * TILES : (b + 1) * TILES], in_=row_sum[:, b * TILES : (b + 1) * TILES]
             )
+            nc.gpsimd.tensor_mul(
+                out=factor[:, b * TILES : (b + 1) * TILES],
+                in0=inv_sum[:, b * TILES : (b + 1) * TILES],
+                in1=mask_f32[:, b * TILES : (b + 1) * TILES],
+            )
 
         def scale_and_store(s):
             b, i = divmod(s, TILES)
-            nc.vector.tensor_scalar(
-                out=out_rows[b][:, i * OUT : (i + 1) * OUT],
-                in0=agg_banks[s][:],
-                scalar1=inv_sum[:, s : s + 1],
-                scalar2=mask_f32[:, s : s + 1],
-                op0=ALU.mult,
-                op1=ALU.mult,
-            )
+            if s in ON_VECTOR_OUT:
+                nc.vector.tensor_scalar(
+                    out=out_rows[b][:, i * OUT : (i + 1) * OUT],
+                    in0=agg_banks[s],
+                    scalar1=inv_sum[:, s : s + 1],
+                    scalar2=mask_f32[:, s : s + 1],
+                    op0=ALU.mult,
+                    op1=ALU.mult,
+                )
+            else:
+                nc.scalar.activation(
+                    out=out_rows[b][:, i * OUT : (i + 1) * OUT],
+                    in_=agg_banks[s],
+                    func=ACT.Copy,
+                    scale=factor[:, s : s + 1],
+                )
             if i % 2 == 1:
                 nc.sync.dma_start(
                     out=out[b].rearrange("(p t) o -> p t o", t=TILES)[:, i - 1 : i + 1, :],
@@ -276,83 +305,104 @@ def tile_graphconvolution_wmask_learnadj_pa_s_kernel(tc, q, k, x, mask, weight, 
         def is_tile(s):
             return 0 <= s < ALL_TILES
 
-        def product_round(s):
-            return max(s + 3, TILES * (s // TILES) + 4)
-
         with tc.manual_schedule():
+            def load_qk(b):
+                nc.sync.dma_start(out=q_rows[b][:], in_=q[b].rearrange("(p t) d -> p (t d)", t=TILES))
+                nc.sync.dma_start(out=k_rows[b][:], in_=k[b].rearrange("(p t) d -> p (t d)", t=TILES))
+
+            def load_w():
+                nc.sync.dma_start(
+                    out=w_rows[:].rearrange("p g (u e) o -> p (g u) (e o)", u=HALVES),
+                    in_=weight.rearrange("(c p e) o -> p c (e o)", p=P, e=2),
+                )
+
             nc.scalar.dma_start(
                 out=mask_bf[:].rearrange("p (b t) -> p b t", b=GRAPHS),
                 in_=mask.rearrange("b (p t) -> p b t", t=TILES),
             )
-            for b in range(GRAPHS):
-                nc.sync.dma_start(out=q_rows[b][:], in_=q[b].rearrange("(p t) d -> p (t d)", t=TILES))
-                nc.sync.dma_start(out=k_rows[b][:], in_=k[b].rearrange("(p t) d -> p (t d)", t=TILES))
+            load_qk(0)
             load_x(0)
             load_x(1)
-            nc.sync.dma_start(
-                out=w_rows[:].rearrange("p g (u e) o -> p (g u) (e o)", u=HALVES),
-                in_=weight.rearrange("(c p e) o -> p c (e o)", p=P, e=2),
-            )
-            for c in range(2, ALL_TILES):
+            load_qk(1)
+            load_x(2)
+            load_x(3)
+            load_w()
+            for c in range(4, ALL_TILES):
                 load_x(c)
 
+            nc.vector.memset(busy_zeros[:].bitcast(F32), 0.0)
+            nc.vector.quantize_mx(out=busy_codes[:].bitcast(FP8X4), scales=busy_scales[:], in_=busy_zeros[:])
             make_identity(nc, ident_bf[:])
             make_identity(nc, ident_f32[:])
+            weight_interleave()
             nc.vector.memset(warm_in[:], 0.0)
-            nc.vector.memset(busy_ones[:], 1.0)
-            nc.vector.quantize_mx(out=busy_codes[:].bitcast(FP8X4), scales=busy_scales[:], in_=busy_ones[:])
-            busy_passes(0, 6)
             nc.scalar.activation(out=warm_out[:], in_=warm_in[:], func=ACT.Exp)
-
-            for b in range(GRAPHS):
-                q_transposes(b)
-                k_transposes(b)
-            x_transposes(0)
-            sim(0)
-            for s in range(1, 3):
-                busy_passes(s, 1)
-                sim(s)
             nc.vector.tensor_copy(out=mask_f32[:], in_=mask_bf[:])
 
-            for r in range(-2, ALL_TILES + 4):
-                c = r + 2
-                if is_tile(r):
+            head_bank = ps_short.tile([P, NODES], F32, tag="bank", name="head_bank")
+            busy_passes(head_bank, 8)
+            q_transposes(0)
+            k_transposes(0)
+            x_transposes(0)
+            sim(0, 0)
+            x_transposes(1)
+            sim(1, 2)
+            x_copy(0)
+            softmax_max(0)
+            x_copy(1)
+            x_quantise(0)
+            softmax_exp(0)
+            q_transposes(1)
+            k_transposes(1)
+            x_transposes(2)
+            softmax_max(1)
+            x_copy(2)
+            x_quantise(1)
+            e_transposes(0)
+            sim(2, 2)
+            for r in range(0, ALL_TILES):
+                if is_tile(r + 3):
+                    x_transposes(r + 3)
+                if r == 4:
+                    support_passes(0)
+                if is_tile(r + 3):
+                    sim(r + 3, 4)
+                if r > 0:
                     softmax_exp(r)
-                if is_tile(c):
-                    x_copy(c)
-                for b in range(GRAPHS):
-                    if r == TILES * b + 3:
-                        support_copy(b)
-
-                if is_tile(c + 1):
-                    x_transposes(c + 1)
-                if is_tile(r):
-                    e_transposes(r)
-                    busy_passes(r + 3, 2)
-                    if is_tile(r + 3):
-                        sim(r + 3)
-
-                if is_tile(r + 1):
-                    softmax_max(r + 1)
-                if r == -1:
-                    weight_quantise()
-                if is_tile(r - 1):
+                if is_tile(r + 3):
+                    x_copy(r + 3)
+                if is_tile(r - 1) and r - 1 in ON_SCALAR_E:
                     e_copy(r - 1)
-                if is_tile(c - 1):
-                    x_quantise(c - 1)
-                for b in range(GRAPHS):
-                    if r == TILES * b + 2:
-                        support_passes(b)
-                    if r == TILES * b + 4:
-                        support_quantise(b)
+                if r == 6:
+                    support_copy(0)
+                if is_tile(r + 2):
+                    softmax_max(r + 2)
+                if is_tile(r - 1) and r - 1 not in ON_SCALAR_E:
+                    e_copy(r - 1)
+                if r == 2:
+                    weight_quantise()
+                if is_tile(r + 2):
+                    x_quantise(r + 2)
+                if r == 7:
+                    support_quantise(0)
+                    invert_sums(0)
                 if is_tile(r - 2):
                     e_quantise(r - 2)
-                for s in range(ALL_TILES):
-                    if product_round(s) == r:
-                        aggregate(s)
-                for b in range(GRAPHS):
-                    if r == TILES * b + 4:
-                        invert_sums(b)
-                for s in range(ALL_TILES):
-                    if product_round(s) + 1 == r:
-                        scale_and_store(s)
+                if r > 0:
+                    e_transposes(r)
+                if r == 6:
+                    support_passes(1)
+            support_copy(1)
+            e_quantise(6)
+            e_copy(7)
+            for s in range(TILES):
+                aggregate(s)
+            for s in range(TILES):
+                scale_and_store(s)
+            invert_sums(1)
+            support_quantise(1)
+            e_quantise(7)
+            for s in range(4, 8):
+                aggregate(s)
+            for s in range(4, 8):
+                scale_and_store(s)

@@ -160,21 +160,21 @@ def tile_graphconvolution_wmask_learnadj_pa_s_kernel(tc, q, k, x, mask, weight, 
                 in_=x_grouped[b][:, j * FEATS : (j + 1) * FEATS],
             )
 
-        def support_passes(b):
-            sup_ps = ps_short.tile([P, TILES, OUT], F32, tag="bank")
-            for j in range(TILES):
-                for g in range(PASSES):
-                    cols = slice((j * PASSES + g) * P, (j * PASSES + g + 1) * P)
-                    nc.tensor.matmul_mx(
-                        out=sup_ps[:, j, :],
-                        lhsT=x_codes[b][:, cols].bitcast(FP8X4),
-                        lhsT_scale=x_scales[b][:, cols],
-                        rhs=w_codes[:, g * OUT : (g + 1) * OUT].bitcast(FP8X4),
-                        rhs_scale=w_scales[:, g * OUT : (g + 1) * OUT],
-                        start=(g == 0),
-                        stop=(g == PASSES - 1),
-                    )
-            sup_banks[b] = sup_ps
+        def support_passes(c):
+            b, j = divmod(c, TILES)
+            if j == 0:
+                sup_banks[b] = ps_short.tile([P, TILES, OUT], F32, tag="bank", name="sup_ps")
+            for g in range(PASSES):
+                cols = slice((j * PASSES + g) * P, (j * PASSES + g + 1) * P)
+                nc.tensor.matmul_mx(
+                    out=sup_banks[b][:, j, :],
+                    lhsT=x_codes[b][:, cols].bitcast(FP8X4),
+                    lhsT_scale=x_scales[b][:, cols],
+                    rhs=w_codes[:, g * OUT : (g + 1) * OUT].bitcast(FP8X4),
+                    rhs_scale=w_scales[:, g * OUT : (g + 1) * OUT],
+                    start=(g == 0),
+                    stop=(g == PASSES - 1),
+                )
 
         def support_copy(b):
             nc.scalar.copy(
@@ -268,14 +268,12 @@ def tile_graphconvolution_wmask_learnadj_pa_s_kernel(tc, q, k, x, mask, weight, 
             )
             agg_banks[s] = agg_ps
 
-        def invert_sums(b):
-            nc.vector.reciprocal(
-                out=inv_sum[:, b * TILES : (b + 1) * TILES], in_=row_sum[:, b * TILES : (b + 1) * TILES]
-            )
+        def invert_sums(first, end):
+            nc.vector.reciprocal(out=inv_sum[:, first:end], in_=row_sum[:, first:end])
+
+        def mask_factors(first, end):
             nc.gpsimd.tensor_mul(
-                out=factor[:, b * TILES : (b + 1) * TILES],
-                in0=inv_sum[:, b * TILES : (b + 1) * TILES],
-                in1=mask_f32[:, b * TILES : (b + 1) * TILES],
+                out=factor[:, first:end], in0=inv_sum[:, first:end], in1=mask_f32[:, first:end]
             )
 
         def scale_and_store(s):
@@ -316,28 +314,26 @@ def tile_graphconvolution_wmask_learnadj_pa_s_kernel(tc, q, k, x, mask, weight, 
                     in_=weight.rearrange("(c p e) o -> p c (e o)", p=P, e=2),
                 )
 
-            nc.scalar.dma_start(
+            load_qk(0)
+            load_x(0)
+            load_w()
+            load_x(1)
+            load_qk(1)
+            for c in range(2, ALL_TILES):
+                load_x(c)
+            nc.sync.dma_start(
                 out=mask_bf[:].rearrange("p (b t) -> p b t", b=GRAPHS),
                 in_=mask.rearrange("b (p t) -> p b t", t=TILES),
             )
-            load_qk(0)
-            load_x(0)
-            load_x(1)
-            load_qk(1)
-            load_x(2)
-            load_x(3)
-            load_w()
-            for c in range(4, ALL_TILES):
-                load_x(c)
 
             nc.vector.memset(busy_zeros[:].bitcast(F32), 0.0)
             nc.vector.quantize_mx(out=busy_codes[:].bitcast(FP8X4), scales=busy_scales[:], in_=busy_zeros[:])
             make_identity(nc, ident_bf[:])
             make_identity(nc, ident_f32[:])
             weight_interleave()
+            nc.gpsimd.tensor_copy(out=mask_f32[:], in_=mask_bf[:])
             nc.vector.memset(warm_in[:], 0.0)
             nc.scalar.activation(out=warm_out[:], in_=warm_in[:], func=ACT.Exp)
-            nc.vector.tensor_copy(out=mask_f32[:], in_=mask_bf[:])
 
             head_bank = ps_short.tile([P, NODES], F32, tag="bank", name="head_bank")
             busy_passes(head_bank, 8)
@@ -345,26 +341,31 @@ def tile_graphconvolution_wmask_learnadj_pa_s_kernel(tc, q, k, x, mask, weight, 
             k_transposes(0)
             x_transposes(0)
             sim(0, 0)
-            x_transposes(1)
             sim(1, 2)
+            x_transposes(1)
             x_copy(0)
             softmax_max(0)
             x_copy(1)
-            x_quantise(0)
             softmax_exp(0)
+            softmax_max(1)
+            x_quantise(0)
             q_transposes(1)
             k_transposes(1)
             x_transposes(2)
-            softmax_max(1)
+            sim(2, 2)
             x_copy(2)
             x_quantise(1)
-            e_transposes(0)
-            sim(2, 2)
             for r in range(0, ALL_TILES):
                 if is_tile(r + 3):
                     x_transposes(r + 3)
+                if r == 0:
+                    e_transposes(0)
+                if r == 3:
+                    for c in range(2):
+                        support_passes(c)
                 if r == 4:
-                    support_passes(0)
+                    for c in range(2, TILES):
+                        support_passes(c)
                 if is_tile(r + 3):
                     sim(r + 3, 4)
                 if r > 0:
@@ -373,34 +374,42 @@ def tile_graphconvolution_wmask_learnadj_pa_s_kernel(tc, q, k, x, mask, weight, 
                     x_copy(r + 3)
                 if is_tile(r - 1) and r - 1 in ON_SCALAR_E:
                     e_copy(r - 1)
-                if r == 6:
+                if r == 5:
                     support_copy(0)
                 if is_tile(r + 2):
                     softmax_max(r + 2)
                 if is_tile(r - 1) and r - 1 not in ON_SCALAR_E:
                     e_copy(r - 1)
-                if r == 2:
+                if r == 1:
                     weight_quantise()
                 if is_tile(r + 2):
                     x_quantise(r + 2)
-                if r == 7:
+                if r == 6:
                     support_quantise(0)
-                    invert_sums(0)
+                    invert_sums(0, TILES)
+                    mask_factors(0, TILES)
                 if is_tile(r - 2):
                     e_quantise(r - 2)
+                if r == 7:
+                    invert_sums(TILES, 7)
+                    mask_factors(TILES, 7)
+                if r == 5:
+                    for c in range(4, 6):
+                        support_passes(c)
+                if r == 6:
+                    for c in range(6, 8):
+                        support_passes(c)
                 if r > 0:
                     e_transposes(r)
-                if r == 6:
-                    support_passes(1)
-            support_copy(1)
-            e_quantise(6)
-            e_copy(7)
             for s in range(TILES):
                 aggregate(s)
+            support_copy(1)
+            e_quantise(6)
             for s in range(TILES):
                 scale_and_store(s)
-            invert_sums(1)
             support_quantise(1)
+            e_copy(7)
+            invert_sums(7, 8)
             e_quantise(7)
             for s in range(4, 8):
                 aggregate(s)

@@ -341,7 +341,7 @@ def tile_graphconvolution_wmask_learnadj_pa_s_kernel(tc, q, k, x, mask, weight, 
             k_transposes(0)
             x_transposes(0)
             sim(0, 0)
-            sim(1, 2)
+            sim(1, 0)
             x_transposes(1)
             x_copy(0)
             softmax_max(0)
@@ -352,7 +352,7 @@ def tile_graphconvolution_wmask_learnadj_pa_s_kernel(tc, q, k, x, mask, weight, 
             q_transposes(1)
             k_transposes(1)
             x_transposes(2)
-            sim(2, 2)
+            sim(2, 0)
             x_copy(2)
             x_quantise(1)
             for r in range(0, ALL_TILES):
@@ -367,7 +367,7 @@ def tile_graphconvolution_wmask_learnadj_pa_s_kernel(tc, q, k, x, mask, weight, 
                     for c in range(2, TILES):
                         support_passes(c)
                 if is_tile(r + 3):
-                    sim(r + 3, 4)
+                    sim(r + 3, 0)
                 if r > 0:
                     softmax_exp(r)
                 if is_tile(r + 3):

import math
from contextlib import ExitStack

import concourse.mybir as mybir
from concourse.masks import make_identity

F32 = mybir.dt.float32
BF16 = mybir.dt.bfloat16
U32 = mybir.dt.uint32
U8 = mybir.dt.uint8
FP8X4 = mybir.dt.float8_e4m3fn_x4
ACT = mybir.ActivationFunctionType
ALU = mybir.AluOpType

P = 128
PACK = 4
GRAPHS, NODES, FEATS, DIM, OUT = 2, 512, 1024, 128, 128
TILES = NODES // P
ON_SCALAR_E = (1, 3)
ON_VECTOR_OUT = (5, 7)
ALL_TILES = GRAPHS * TILES
PASSES = FEATS // (P * PACK)
BUSY_N = 128
HALVES = 2
SCALE = 1.0 / math.sqrt(DIM)

FLOPS = 2 * GRAPHS * NODES * (NODES * DIM + FEATS * OUT + NODES * OUT)


def tile_graphconvolution_wmask_learnadj_pa_s_kernel(tc, q, k, x, mask, weight, out):
    nc = tc.nc
    with ExitStack() as ctx:
        keep = ctx.enter_context(tc.tile_pool(name="keep", bufs=1))
        e_pool = ctx.enter_context(tc.tile_pool(name="e_pool", bufs=3))
        ps_sim = ctx.enter_context(tc.psum_pool(name="ps_sim", bufs=2))
        ps_short = ctx.enter_context(tc.psum_pool(name="ps_short", bufs=6))

        q_rows = [keep.tile([P, TILES * DIM], BF16, name="q_rows%d" % b) for b in range(GRAPHS)]
        k_rows = [keep.tile([P, TILES * DIM], BF16, name="k_rows%d" % b) for b in range(GRAPHS)]
        x_rows = [keep.tile([P, TILES * FEATS], BF16, name="x_rows%d" % b) for b in range(GRAPHS)]
        w_rows = keep.tile([P, PASSES, PACK, OUT], BF16, name="w_rows")
        mask_bf = keep.tile([P, ALL_TILES], BF16, name="mask_bf")

        qT = [keep.tile([P, NODES], BF16, name="qT%d" % b) for b in range(GRAPHS)]
        kT = [keep.tile([P, NODES], BF16, name="kT%d" % b) for b in range(GRAPHS)]

        w_grouped = keep.tile([P, PASSES * OUT * PACK], BF16, name="w_grouped", align_bytes=64)
        w_codes = keep.tile([P, PASSES * OUT], U32, name="w_codes", align_bytes=64)
        w_scales = keep.tile([P, PASSES * OUT], U8, name="w_scales", align_bytes=64)

        x_grouped = [
            keep.tile([P, TILES * FEATS], BF16, name="x_grouped%d" % b, align_bytes=64)
            for b in range(GRAPHS)
        ]
        x_codes = [
            keep.tile([P, TILES * FEATS // PACK], U32, name="x_codes%d" % b, align_bytes=64)
            for b in range(GRAPHS)
        ]
        x_scales = [
            keep.tile([P, TILES * FEATS // PACK], U8, name="x_scales%d" % b, align_bytes=64)
            for b in range(GRAPHS)
        ]

        s_grouped = [
            keep.tile([P, OUT * PACK], BF16, name="s_grouped%d" % b, align_bytes=64)
            for b in range(GRAPHS)
        ]
        s_codes = [keep.tile([P, OUT], U32, name="s_codes%d" % b, align_bytes=64) for b in range(GRAPHS)]
        s_scales = [keep.tile([P, OUT], U8, name="s_scales%d" % b, align_bytes=64) for b in range(GRAPHS)]

        e_grouped = [
            keep.tile([P, NODES * PACK], BF16, name="e_grouped%d" % b, align_bytes=64)
            for b in range(GRAPHS)
        ]
        e_codes = [keep.tile([P, NODES], U32, name="e_codes%d" % b, align_bytes=64) for b in range(GRAPHS)]
        e_scales = [keep.tile([P, NODES], U8, name="e_scales%d" % b, align_bytes=64) for b in range(GRAPHS)]

        scaled_sim = keep.tile([P, ALL_TILES * NODES], F32, name="scaled_sim")
        exp_bias = keep.tile([P, ALL_TILES], F32, name="exp_bias")
        row_sum = keep.tile([P, ALL_TILES], F32, name="row_sum")
        inv_sum = keep.tile([P, ALL_TILES], F32, name="inv_sum")
        factor = keep.tile([P, ALL_TILES], F32, name="factor")
        mask_f32 = keep.tile([P, ALL_TILES], F32, name="mask_f32")
        out_rows = [keep.tile([P, TILES * OUT], F32, name="out_rows%d" % b) for b in range(GRAPHS)]

        ident_bf = keep.tile([P, P], BF16, name="ident_bf")
        ident_f32 = keep.tile([P, P], F32, name="ident_f32")
        busy_zeros = keep.tile([P, BUSY_N * PACK], BF16, name="busy_zeros", align_bytes=64)
        busy_codes = keep.tile([P, BUSY_N], U32, name="busy_codes", align_bytes=64)
        busy_scales = keep.tile([P, BUSY_N], U8, name="busy_scales", align_bytes=64)
        warm_in = keep.tile([P, 1], F32, name="warm_in")
        warm_out = keep.tile([P, 1], F32, name="warm_out")

        xT_banks = {}
        sim_banks = {}
        e_tiles = {}
        eT_banks = {}
        sup_banks = {}
        agg_banks = {}

        def load_x(c):
            b, j = divmod(c, TILES)
            nc.sync.dma_start(
                out=x_rows[b][:, j * FEATS : (j + 1) * FEATS],
                in_=x[b].rearrange("(p t) f -> p t f", t=TILES)[:, j, :],
            )

        def q_transposes(b):
            qT_ps = ps_short.tile([P, TILES, P], BF16, tag="bank")
            for t in range(TILES):
                nc.tensor.transpose(qT_ps[:, t, :], q_rows[b][:, t * DIM : (t + 1) * DIM], ident_bf[:])
            nc.scalar.copy(out=qT[b][:], in_=qT_ps[:].rearrange("d t p -> d (t p)"))

        def k_transposes(b):
            kT_ps = ps_short.tile([P, TILES, P], BF16, tag="bank")
            for t in range(TILES):
                nc.tensor.transpose(kT_ps[:, t, :], k_rows[b][:, t * DIM : (t + 1) * DIM], ident_bf[:])
            nc.vector.tensor_copy(
                out=kT[b][:].rearrange("d (u p e) -> d u p e", u=HALVES, e=2),
                in_=kT_ps[:].rearrange("d (u e) p -> d u p e", u=HALVES),
            )

        def weight_interleave():
            nc.gpsimd.tensor_scalar(
                out=w_grouped[:].rearrange("p (g o t) -> p g o t", g=PASSES, t=PACK),
                in0=w_rows[:].rearrange("p g t o -> p g o t"),
                scalar1=1.0,
                scalar2=0.0,
                op0=ALU.mult,
                op1=ALU.add,
            )

        def weight_quantise():
            nc.vector.quantize_mx(out=w_codes[:].bitcast(FP8X4), scales=w_scales[:], in_=w_grouped[:])

        def x_transposes(c):
            b, j = divmod(c, TILES)
            words = x_rows[b][:].bitcast(F32)
            xT_ps = ps_short.tile([P, PASSES * HALVES, P], F32, tag="bank")
            for w in range(PASSES * HALVES):
                first = (j * PASSES * HALVES + w) * P
                nc.tensor.transpose(xT_ps[:, w, :], words[:, first : first + P], ident_f32[:])
            xT_banks[c] = xT_ps

        def x_copy(c):
            b, j = divmod(c, TILES)
            grouped_words = x_grouped[b][:].bitcast(F32).rearrange(
                "p (j g m u) -> p j g m u", j=TILES, g=PASSES, u=HALVES
            )
            nc.scalar.copy(
                out=grouped_words[:, j],
                in_=xT_banks[c][:].rearrange("p (g u) m -> p g m u", u=HALVES),
            )

        def x_quantise(c):
            b, j = divmod(c, TILES)
            nc.vector.quantize_mx(
                out=x_codes[b][:, j * FEATS // PACK : (j + 1) * FEATS // PACK].bitcast(FP8X4),
                scales=x_scales[b][:, j * FEATS // PACK : (j + 1) * FEATS // PACK],
                in_=x_grouped[b][:, j * FEATS : (j + 1) * FEATS],
            )

        def support_passes(c):
            b, j = divmod(c, TILES)
            if j == 0:
                sup_banks[b] = ps_short.tile([P, TILES, OUT], F32, tag="bank", name="sup_ps")
            for g in range(PASSES):
                cols = slice((j * PASSES + g) * P, (j * PASSES + g + 1) * P)
                nc.tensor.matmul_mx(
                    out=sup_banks[b][:, j, :],
                    lhsT=x_codes[b][:, cols].bitcast(FP8X4),
                    lhsT_scale=x_scales[b][:, cols],
                    rhs=w_codes[:, g * OUT : (g + 1) * OUT].bitcast(FP8X4),
                    rhs_scale=w_scales[:, g * OUT : (g + 1) * OUT],
                    start=(g == 0),
                    stop=(g == PASSES - 1),
                )

        def support_copy(b):
            nc.scalar.copy(
                out=s_grouped[b][:].rearrange("p (o j) -> p o j", j=PACK),
                in_=sup_banks[b][:].rearrange("p j o -> p o j"),
            )

        def support_quantise(b):
            nc.vector.quantize_mx(out=s_codes[b][:].bitcast(FP8X4), scales=s_scales[b][:], in_=s_grouped[b][:])

        def busy_passes(bank, count):
            for repeat in range(count):
                nc.tensor.matmul_mx(
                    out=bank[:, :BUSY_N],
                    lhsT=busy_codes[:, :P].bitcast(FP8X4),
                    lhsT_scale=busy_scales[:, :P],
                    rhs=busy_codes[:].bitcast(FP8X4),
                    rhs_scale=busy_scales[:],
                    start=True,
                    stop=True,
                )

        def sim(s, busy):
            b, i = divmod(s, TILES)
            sim_ps = ps_sim.tile([P, NODES], F32, tag="bank")
            busy_passes(sim_ps, busy)
            nc.tensor.matmul(sim_ps[:], lhsT=qT[b][:, i * P : (i + 1) * P], rhs=kT[b][:], start=True, stop=True)
            sim_banks[s] = sim_ps

        def softmax_max(s):
            nc.vector.tensor_scalar(
                out=scaled_sim[:, s * NODES : (s + 1) * NODES],
                in0=sim_banks[s][:],
                scalar1=-SCALE,
                scalar2=None,
                op0=ALU.mult,
                op1=ALU.min,
                accum_out=exp_bias[:, s : s + 1],
            )

        def softmax_exp(s):
            e_rows = e_pool.tile([P, NODES], BF16, tag="e_rows")
            nc.scalar.activation(
                out=e_rows[:],
                in_=scaled_sim[:, s * NODES : (s + 1) * NODES],
                func=ACT.Exp,
                bias=exp_bias[:, s : s + 1],
                scale=-1.0,
                accum_out=row_sum[:, s : s + 1],
            )
            e_tiles[s] = e_rows

        def e_transposes(s):
            words = e_tiles[s][:].bitcast(F32)
            eT_ps = ps_short.tile([P, HALVES, P], F32, tag="bank")
            for u in range(HALVES):
                nc.tensor.transpose(eT_ps[:, u, :], words[:, u * P : (u + 1) * P], ident_f32[:])
            eT_banks[s] = eT_ps

        def e_copy(s):
            b, i = divmod(s, TILES)
            copy = nc.scalar.copy if s in ON_SCALAR_E else nc.vector.tensor_copy
            grouped_words = e_grouped[b][:].bitcast(F32).rearrange("p (i n u) -> p i n u", i=TILES, u=HALVES)
            source = eT_banks[s][:].rearrange("p u n -> p n u")
            copy(out=grouped_words[:, i], in_=source)

        def e_quantise(s):
            b, i = divmod(s, TILES)
            nc.vector.quantize_mx(
                out=e_codes[b][:, i * P : (i + 1) * P].bitcast(FP8X4),
                scales=e_scales[b][:, i * P : (i + 1) * P],
                in_=e_grouped[b][:, i * P * PACK : (i + 1) * P * PACK],
            )

        def aggregate(s):
            b, i = divmod(s, TILES)
            if s < TILES:
                if s == 0:
                    agg_banks["first"] = ps_short.tile([P, TILES, OUT], F32, tag="bank", name="agg_ps")
                agg_ps = agg_banks["first"][:, i, :]
            else:
                agg_ps = ps_short.tile([P, OUT], F32, tag="bank", name="agg_one")[:]
            nc.tensor.matmul_mx(
                out=agg_ps,
                lhsT=e_codes[b][:, i * P : (i + 1) * P].bitcast(FP8X4),
                lhsT_scale=e_scales[b][:, i * P : (i + 1) * P],
                rhs=s_codes[b][:].bitcast(FP8X4),
                rhs_scale=s_scales[b][:],
                start=True,
                stop=True,
            )
            agg_banks[s] = agg_ps

        def invert_sums(first, end):
            nc.vector.reciprocal(out=inv_sum[:, first:end], in_=row_sum[:, first:end])

        def mask_factors(first, end):
            nc.gpsimd.tensor_mul(
                out=factor[:, first:end], in0=inv_sum[:, first:end], in1=mask_f32[:, first:end]
            )

        def scale_and_store(s):
            b, i = divmod(s, TILES)
            if s in ON_VECTOR_OUT:
                nc.vector.tensor_scalar(
                    out=out_rows[b][:, i * OUT : (i + 1) * OUT],
                    in0=agg_banks[s],
                    scalar1=inv_sum[:, s : s + 1],
                    scalar2=mask_f32[:, s : s + 1],
                    op0=ALU.mult,
                    op1=ALU.mult,
                )
            else:
                nc.scalar.activation(
                    out=out_rows[b][:, i * OUT : (i + 1) * OUT],
                    in_=agg_banks[s],
                    func=ACT.Copy,
                    scale=factor[:, s : s + 1],
                )
            if i % 2 == 1:
                nc.sync.dma_start(
                    out=out[b].rearrange("(p t) o -> p t o", t=TILES)[:, i - 1 : i + 1, :],
                    in_=out_rows[b][:, (i - 1) * OUT : (i + 1) * OUT].rearrange("p (t o) -> p t o", t=2),
                )

        def is_tile(s):
            return 0 <= s < ALL_TILES

        with tc.manual_schedule():
            def load_qk(b):
                nc.sync.dma_start(out=q_rows[b][:], in_=q[b].rearrange("(p t) d -> p (t d)", t=TILES))
                nc.sync.dma_start(out=k_rows[b][:], in_=k[b].rearrange("(p t) d -> p (t d)", t=TILES))

            def load_w():
                nc.sync.dma_start(
                    out=w_rows[:].rearrange("p g (u e) o -> p (g u) (e o)", u=HALVES),
                    in_=weight.rearrange("(c p e) o -> p c (e o)", p=P, e=2),
                )

            load_qk(0)
            load_x(0)
            load_w()
            load_x(1)
            load_qk(1)
            for c in range(2, ALL_TILES):
                load_x(c)
            nc.sync.dma_start(
                out=mask_bf[:].rearrange("p (b t) -> p b t", b=GRAPHS),
                in_=mask.rearrange("b (p t) -> p b t", t=TILES),
            )

            nc.vector.memset(busy_zeros[:].bitcast(F32), 0.0)
            nc.vector.quantize_mx(out=busy_codes[:].bitcast(FP8X4), scales=busy_scales[:], in_=busy_zeros[:])
            make_identity(nc, ident_bf[:])
            make_identity(nc, ident_f32[:])
            weight_interleave()
            nc.gpsimd.tensor_copy(out=mask_f32[:], in_=mask_bf[:])
            nc.vector.memset(warm_in[:], 0.0)
            nc.scalar.activation(out=warm_out[:], in_=warm_in[:], func=ACT.Exp)

            head_bank = ps_short.tile([P, NODES], F32, tag="bank", name="head_bank")
            busy_passes(head_bank, 8)
            q_transposes(0)
            k_transposes(0)
            x_transposes(0)
            sim(0, 0)
            sim(1, 0)
            x_transposes(1)
            x_copy(0)
            softmax_max(0)
            x_copy(1)
            softmax_exp(0)
            softmax_max(1)
            x_quantise(0)
            q_transposes(1)
            k_transposes(1)
            x_transposes(2)
            sim(2, 0)
            x_copy(2)
            x_quantise(1)
            for r in range(0, ALL_TILES):
                if is_tile(r + 3):
                    x_transposes(r + 3)
                if r == 0:
                    e_transposes(0)
                if r == 3:
                    for c in range(2):
                        support_passes(c)
                if r == 4:
                    for c in range(2, TILES):
                        support_passes(c)
                if is_tile(r + 3):
                    sim(r + 3, 0)
                if r > 0:
                    softmax_exp(r)
                if is_tile(r + 3):
                    x_copy(r + 3)
                if is_tile(r - 1) and r - 1 in ON_SCALAR_E:
                    e_copy(r - 1)
                if r == 5:
                    support_copy(0)
                if is_tile(r + 2):
                    softmax_max(r + 2)
                if is_tile(r - 1) and r - 1 not in ON_SCALAR_E:
                    e_copy(r - 1)
                if r == 1:
                    weight_quantise()
                if is_tile(r + 2):
                    x_quantise(r + 2)
                if r == 6:
                    support_quantise(0)
                    invert_sums(0, TILES)
                    mask_factors(0, TILES)
                if is_tile(r - 2):
                    e_quantise(r - 2)
                if r == 7:
                    invert_sums(TILES, 7)
                    mask_factors(TILES, 7)
                if r == 5:
                    for c in range(4, 6):
                        support_passes(c)
                if r == 6:
                    for c in range(6, 8):
                        support_passes(c)
                if r > 0:
                    e_transposes(r)
            for s in range(TILES):
                aggregate(s)
            support_copy(1)
            e_quantise(6)
            for s in range(TILES):
                scale_and_store(s)
            support_quantise(1)
            e_copy(7)
            invert_sums(7, 8)
            e_quantise(7)
            for s in range(4, 8):
                aggregate(s)
            for s in range(4, 8):
                scale_and_store(s)
